import numpy as np
import ml_dtypes


def mxq(x, axis, fmt="e4m3"):
    dtype, down = {"e4m3": (ml_dtypes.float8_e4m3fn, 7), "e5m2": (ml_dtypes.float8_e5m2, 14)}[fmt]
    v = np.moveaxis(np.asarray(x, np.float32).astype(ml_dtypes.bfloat16).astype(np.float64), axis, -1)
    blocks = v.reshape(v.shape[:-1] + (-1, 32))
    amax = np.abs(blocks).max(-1, keepdims=True)
    byte = np.maximum(np.where(amax > 0, np.frexp(amax)[1] - 1 + 127, 0) - down, 1)
    scale = np.exp2(byte - 127.0)
    codes = (blocks / scale).astype(np.float32).astype(dtype).astype(np.float64)
    return np.moveaxis((codes * scale).reshape(v.shape), -1, axis)


WIDE = False


def mx_kscale(k):
    if not WIDE:
        return np.ones(k)
    levels = np.array([10, -10, 5, -5, 0])
    a = np.random.permutation(np.resize(levels, k // 512 * 4)).reshape(k // 512, 4)
    idx = np.arange(k)
    return np.exp2(a[idx // 512, idx % 128 // 32])


BF16 = ml_dtypes.bfloat16


def bf(x):
    return np.asarray(x, np.float32).astype(BF16)


def f64(x):
    return np.asarray(x).astype(np.float64)


B, T, D, H = 4, 1024, 1024, 8
HD = D // H
SCALE = HD ** (-0.5)


def rotate_half(u):
    u1, u2 = np.split(u, 2, axis=-1)
    return np.concatenate([-u2, u1], axis=-1)


def apply_rope(u, sin, cos):
    return u * cos[None, :, None, :] + rotate_half(u) * sin[None, :, None, :]


def setup_inputs():
    s = mx_kscale(D)
    return {"x": bf(np.random.standard_normal((B, T, D)) * s),
            "sin": bf(np.random.standard_normal((T, HD))),
            "cos": bf(np.random.standard_normal((T, HD))),
            "W_qkv": bf(np.random.standard_normal((D, D + 2 * HD)) * 2.0 / np.sqrt(D) / s[:, None])}


def reference(x, sin, cos, W_qkv):
    sin, cos = f64(sin), f64(cos)
    qkv = mxq(f64(x), 2, "e4m3") @ mxq(f64(W_qkv), 0, "e4m3")
    q, k, v = np.split(qkv, [D, D + HD], axis=-1)
    q = q.reshape(B, T, H, HD) * SCALE
    q_rot = np.ascontiguousarray(apply_rope(q, sin, cos).transpose(0, 2, 1, 3))
    k_rot = apply_rope(k[:, :, None, :], sin, cos)[:, :, 0, :]
    return q_rot, k_rot, v

@@ -1,0 +1,207 @@
+from contextlib import ExitStack
+
+import concourse.mybir as mybir
+from concourse.masks import make_identity
+
+F32 = mybir.dt.float32
+BF16 = mybir.dt.bfloat16
+U32 = mybir.dt.uint32
+U8 = mybir.dt.uint8
+FP8X4 = mybir.dt.float8_e4m3fn_x4
+MULT = mybir.AluOpType.mult
+ADD = mybir.AluOpType.add
+
+P = 128
+BATCH = 4
+SEQ = 1024
+D_MODEL = 1024
+HEADS = 8
+HEAD_DIM = 128
+HALF = HEAD_DIM // 2
+Q_SCALE = HEAD_DIM**-0.5
+N_QKV = D_MODEL + 2 * HEAD_DIM
+
+PACK = 4
+K_PASS = P * PACK
+PASSES = D_MODEL // K_PASS
+WORDS = D_MODEL // 2
+
+TILES = 4
+GROUP = TILES * P
+GROUPS_PER_BATCH = SEQ // GROUP
+N_GROUPS = BATCH * GROUPS_PER_BATCH
+N_TILES = N_GROUPS * TILES
+AHEAD = 2
+
+COL_LOWER = 0
+COL_UPPER = HEADS * HALF
+COL_K = D_MODEL
+COL_V = D_MODEL + HEAD_DIM
+
+ROW_K = HEADS
+ROW_V = HEADS + 1
+
+LOWER = slice(0, HALF)
+UPPER = slice(HALF, HEAD_DIM)
+
+FLOPS = 2 * BATCH * SEQ * D_MODEL * N_QKV
+
+
+def over_heads(table_half):
+    return table_half.unsqueeze(1).to_broadcast([P, HEADS, HALF])
+
+
+def tile_multiqueryattention_pa_t_kernel(tc, x, sin, cos, w_qkv, q_rot, k_rot, v_out):
+    nc = tc.nc
+    with ExitStack() as ctx:
+        consts = ctx.enter_context(tc.tile_pool(name="consts", bufs=1))
+        x_pool = ctx.enter_context(tc.tile_pool(name="x_pool", bufs=N_GROUPS))
+        x_stage = ctx.enter_context(tc.tile_pool(name="x_stage", bufs=2 * AHEAD))
+        psum_t = ctx.enter_context(tc.psum_pool(name="psum_t", bufs=2))
+        psum_q = ctx.enter_context(tc.psum_pool(name="psum_q", bufs=2))
+        psum_kv = ctx.enter_context(tc.psum_pool(name="psum_kv", bufs=1))
+
+        cos_sb = consts.tile([P, GROUPS_PER_BATCH, TILES, HEAD_DIM], BF16)
+        sin_sb = consts.tile([P, GROUPS_PER_BATCH, TILES, HEAD_DIM], BF16)
+        nc.scalar.dma_start(out=cos_sb[:], in_=cos.rearrange("(s p i) d -> p s i d", p=P, i=TILES))
+        nc.scalar.dma_start(out=sin_sb[:], in_=sin.rearrange("(s p i) d -> p s i d", p=P, i=TILES))
+
+        x_tiles = []
+
+        def load_x(group):
+            b, s = divmod(group, GROUPS_PER_BATCH)
+            x_sb = x_pool.tile([P, TILES * D_MODEL], BF16)
+            rows = x[b, s * GROUP : (s + 1) * GROUP, :]
+            nc.sync.dma_start(out=x_sb[:], in_=rows.rearrange("(p i) k -> p (i k)", i=TILES))
+            x_tiles.append(x_sb)
+
+        identity = consts.tile([P, P], F32)
+        make_identity(nc, identity[:])
+
+        def transpose_and_quantise(n):
+            group, i = divmod(n, TILES)
+            x_words = x_tiles[group][:].bitcast(F32)
+            xt = psum_t.tile([P, PASSES * 2, P], F32)
+            for j in range(PASSES * 2):
+                first = i * WORDS + j * P
+                nc.tensor.transpose(out=xt[:, j, :], in_=x_words[:, first : first + P], identity=identity[:])
+            grouped = x_stage.tile([P, PASSES * P * PACK], BF16, align_bytes=64)
+            nc.scalar.copy(
+                out=grouped[:].bitcast(F32).rearrange("p (g r u) -> p g r u", g=PASSES, u=2),
+                in_=xt[:].rearrange("p (g u) r -> p g r u", u=2),
+            )
+            codes = x_stage.tile([P, PASSES * P], U32, align_bytes=64)
+            scales = x_stage.tile([P, PASSES * P], U8, align_bytes=64)
+            nc.vector.quantize_mx(out=codes[:].bitcast(FP8X4), scales=scales[:], in_=grouped[:])
+            return codes, scales
+
+        w_codes = consts.tile([P, PASSES, N_QKV], U32, align_bytes=64)
+        w_scales = consts.tile([P, PASSES, N_QKV], U8, align_bytes=64)
+
+        x_mx = {}
+        with tc.tile_pool(name="w_stage", bufs=1) as w_stage:
+            w_raw = w_stage.tile([P, PASSES, PACK, N_QKV], BF16)
+            for g in range(PASSES):
+                rows = w_qkv[g * K_PASS : (g + 1) * K_PASS, :]
+                nc.sync.dma_start(
+                    out=w_raw[:, g, :, :].rearrange("p (u e) c -> p u e c", u=2),
+                    in_=rows.rearrange("(u p e) c -> p u e c", u=2, e=2),
+                )
+            for group in range(N_GROUPS):
+                load_x(group)
+
+            w_grouped = w_stage.tile([P, PASSES, N_QKV, PACK], BF16, align_bytes=64)
+            for g in range(PASSES):
+                q_halves = w_raw[:, g, :, 0:D_MODEL].rearrange("p t (h two d) -> p two h d t", two=2, d=HALF)
+                nc.vector.tensor_copy(
+                    out=w_grouped[:, g, COL_LOWER:COL_UPPER, :].rearrange("p (h d) t -> p h d t", d=HALF),
+                    in_=q_halves[:, 0],
+                )
+                nc.scalar.copy(
+                    out=w_grouped[:, g, COL_UPPER:COL_K, :].rearrange("p (h d) t -> p h d t", d=HALF),
+                    in_=q_halves[:, 1],
+                )
+                nc.vector.tensor_copy(
+                    out=w_grouped[:, g, COL_K:N_QKV, :],
+                    in_=w_raw[:, g, :, COL_K:N_QKV].rearrange("p t c -> p c t"),
+                )
+                for cols in (slice(COL_LOWER, COL_UPPER), slice(COL_K, N_QKV), slice(COL_UPPER, COL_K)):
+                    nc.vector.quantize_mx(
+                        out=w_codes[:, g, cols].bitcast(FP8X4),
+                        scales=w_scales[:, g, cols],
+                        in_=w_grouped[:, g, cols, :].rearrange("p c t -> p (c t)"),
+                    )
+
+            for n in range(AHEAD):
+                x_mx[n] = transpose_and_quantise(n)
+
+        out_pool = ctx.enter_context(tc.tile_pool(name="out_pool", bufs=3))
+        side_pool = ctx.enter_context(tc.tile_pool(name="side_pool", bufs=3))
+
+        def times_table(out, bank, factor, table):
+            nc.vector.scalar_tensor_tensor(out=out, in0=bank, scalar=factor, in1=table, op0=MULT, op1=MULT)
+
+        def project(n, bank, col, width):
+            codes, scales = x_mx[n]
+            for g in range(PASSES):
+                tokens = slice(g * P, (g + 1) * P)
+                nc.tensor.matmul_mx(
+                    out=bank,
+                    lhsT=codes[:, tokens].bitcast(FP8X4),
+                    lhsT_scale=scales[:, tokens],
+                    rhs=w_codes[:, g, col : col + width].bitcast(FP8X4),
+                    rhs_scale=w_scales[:, g, col : col + width],
+                    start=(g == 0),
+                    stop=(g == PASSES - 1),
+                )
+
+        for group in range(N_GROUPS):
+            b, s = divmod(group, GROUPS_PER_BATCH)
+            result = out_pool.tile([P, HEADS + 2, TILES, HEAD_DIM], F32)
+            bank_k = psum_kv.tile([P, TILES, HEAD_DIM], F32)
+            bank_v = psum_kv.tile([P, TILES, HEAD_DIM], F32)
+
+            for i in range(TILES):
+                n = group * TILES + i
+                if n % AHEAD == 0:
+                    for later in range(n + AHEAD, min(n + 2 * AHEAD, N_TILES)):
+                        x_mx[later] = transpose_and_quantise(later)
+
+                bank_lower = psum_q.tile([P, HEADS * HALF], F32)
+                bank_upper = psum_q.tile([P, HEADS * HALF], F32)
+                project(n, bank_lower[:], COL_LOWER, HEADS * HALF)
+                project(n, bank_upper[:], COL_UPPER, HEADS * HALF)
+                project(n, bank_k[:, i, :], COL_K, HEAD_DIM)
+                project(n, bank_v[:, i, :], COL_V, HEAD_DIM)
+
+                lower = bank_lower[:].rearrange("p (h d) -> p h d", d=HALF)
+                upper = bank_upper[:].rearrange("p (h d) -> p h d", d=HALF)
+                side = side_pool.tile([P, HEADS, HEAD_DIM], F32)
+                times_table(result[:, 0:HEADS, i, LOWER], lower, Q_SCALE, over_heads(cos_sb[:, s, i, LOWER]))
+                times_table(side[:, :, UPPER], lower, Q_SCALE, over_heads(sin_sb[:, s, i, UPPER]))
+                times_table(result[:, 0:HEADS, i, UPPER], upper, Q_SCALE, over_heads(cos_sb[:, s, i, UPPER]))
+                times_table(side[:, :, LOWER], upper, -Q_SCALE, over_heads(sin_sb[:, s, i, LOWER]))
+                nc.gpsimd.tensor_tensor(
+                    out=result[:, 0:HEADS, i, :], in0=result[:, 0:HEADS, i, :], in1=side[:], op=ADD
+                )
+
+            side_k = side_pool.tile([P, TILES, HEAD_DIM], F32)
+            times_table(result[:, ROW_K, :, :], bank_k[:], 1.0, cos_sb[:, s, :, :])
+            times_table(side_k[:, :, LOWER], bank_k[:, :, UPPER], -1.0, sin_sb[:, s, :, LOWER])
+            times_table(side_k[:, :, UPPER], bank_k[:, :, LOWER], 1.0, sin_sb[:, s, :, UPPER])
+            nc.gpsimd.tensor_tensor(out=result[:, ROW_K, :, :], in0=result[:, ROW_K, :, :], in1=side_k[:], op=ADD)
+            nc.scalar.copy(out=result[:, ROW_V, :, :], in_=bank_v[:])
+
+            positions = slice(s * GROUP, (s + 1) * GROUP)
+            nc.sync.dma_start(
+                out=q_rot[b, :, positions, :].rearrange("h (p i) d -> p h (i d)", i=TILES),
+                in_=result[:, 0:HEADS, :, :].rearrange("p h i d -> p h (i d)"),
+            )
+            nc.sync.dma_start(
+                out=k_rot[b, positions, :].rearrange("(p i) d -> p (i d)", i=TILES),
+                in_=result[:, ROW_K, :, :].rearrange("p i d -> p (i d)"),
+            )
+            nc.sync.dma_start(
+                out=v_out[b, positions, :].rearrange("(p i) d -> p (i d)", i=TILES),
+                in_=result[:, ROW_V, :, :].rearrange("p i d -> p (i d)"),
+            )

@@ -26,12 +26,12 @@ K_PASS = P * PACK
 PASSES = D_MODEL // K_PASS
 WORDS = D_MODEL // 2
 
-TILES = 4
+TILES = 2
 GROUP = TILES * P
 GROUPS_PER_BATCH = SEQ // GROUP
 N_GROUPS = BATCH * GROUPS_PER_BATCH
-N_TILES = N_GROUPS * TILES
-AHEAD = 2
+
+VECTOR_ADD_PERIOD = 16
 
 COL_LOWER = 0
 COL_UPPER = HEADS * HALF
@@ -56,8 +56,8 @@ def tile_multiqueryattention_pa_t_kernel(tc, x, sin, cos, w_qkv, q_rot, k_rot, v
     with ExitStack() as ctx:
         consts = ctx.enter_context(tc.tile_pool(name="consts", bufs=1))
         x_pool = ctx.enter_context(tc.tile_pool(name="x_pool", bufs=N_GROUPS))
-        x_stage = ctx.enter_context(tc.tile_pool(name="x_stage", bufs=2 * AHEAD))
-        psum_t = ctx.enter_context(tc.psum_pool(name="psum_t", bufs=2))
+        x_stage = ctx.enter_context(tc.tile_pool(name="x_stage", bufs=3))
+        psum_t = ctx.enter_context(tc.psum_pool(name="psum_t", bufs=TILES))
         psum_q = ctx.enter_context(tc.psum_pool(name="psum_q", bufs=2))
         psum_kv = ctx.enter_context(tc.psum_pool(name="psum_kv", bufs=1))
 
@@ -66,39 +66,13 @@ def tile_multiqueryattention_pa_t_kernel(tc, x, sin, cos, w_qkv, q_rot, k_rot, v
         nc.scalar.dma_start(out=cos_sb[:], in_=cos.rearrange("(s p i) d -> p s i d", p=P, i=TILES))
         nc.scalar.dma_start(out=sin_sb[:], in_=sin.rearrange("(s p i) d -> p s i d", p=P, i=TILES))
 
-        x_tiles = []
-
-        def load_x(group):
-            b, s = divmod(group, GROUPS_PER_BATCH)
-            x_sb = x_pool.tile([P, TILES * D_MODEL], BF16)
-            rows = x[b, s * GROUP : (s + 1) * GROUP, :]
-            nc.sync.dma_start(out=x_sb[:], in_=rows.rearrange("(p i) k -> p (i k)", i=TILES))
-            x_tiles.append(x_sb)
-
         identity = consts.tile([P, P], F32)
         make_identity(nc, identity[:])
 
-        def transpose_and_quantise(n):
-            group, i = divmod(n, TILES)
-            x_words = x_tiles[group][:].bitcast(F32)
-            xt = psum_t.tile([P, PASSES * 2, P], F32)
-            for j in range(PASSES * 2):
-                first = i * WORDS + j * P
-                nc.tensor.transpose(out=xt[:, j, :], in_=x_words[:, first : first + P], identity=identity[:])
-            grouped = x_stage.tile([P, PASSES * P * PACK], BF16, align_bytes=64)
-            nc.scalar.copy(
-                out=grouped[:].bitcast(F32).rearrange("p (g r u) -> p g r u", g=PASSES, u=2),
-                in_=xt[:].rearrange("p (g u) r -> p g r u", u=2),
-            )
-            codes = x_stage.tile([P, PASSES * P], U32, align_bytes=64)
-            scales = x_stage.tile([P, PASSES * P], U8, align_bytes=64)
-            nc.vector.quantize_mx(out=codes[:].bitcast(FP8X4), scales=scales[:], in_=grouped[:])
-            return codes, scales
-
         w_codes = consts.tile([P, PASSES, N_QKV], U32, align_bytes=64)
         w_scales = consts.tile([P, PASSES, N_QKV], U8, align_bytes=64)
+        x_tiles = []
 
-        x_mx = {}
         with tc.tile_pool(name="w_stage", bufs=1) as w_stage:
             w_raw = w_stage.tile([P, PASSES, PACK, N_QKV], BF16)
             for g in range(PASSES):
@@ -108,7 +82,11 @@ def tile_multiqueryattention_pa_t_kernel(tc, x, sin, cos, w_qkv, q_rot, k_rot, v
                     in_=rows.rearrange("(u p e) c -> p u e c", u=2, e=2),
                 )
             for group in range(N_GROUPS):
-                load_x(group)
+                b, s = divmod(group, GROUPS_PER_BATCH)
+                x_sb = x_pool.tile([P, TILES * D_MODEL], BF16)
+                rows = x[b, s * GROUP : (s + 1) * GROUP, :]
+                nc.sync.dma_start(out=x_sb[:], in_=rows.rearrange("(p i) k -> p (i k)", i=TILES))
+                x_tiles.append(x_sb)
 
             w_grouped = w_stage.tile([P, PASSES, N_QKV, PACK], BF16, align_bytes=64)
             for g in range(PASSES):
@@ -132,65 +110,85 @@ def tile_multiqueryattention_pa_t_kernel(tc, x, sin, cos, w_qkv, q_rot, k_rot, v
                         in_=w_grouped[:, g, cols, :].rearrange("p c t -> p (c t)"),
                     )
 
-            for n in range(AHEAD):
-                x_mx[n] = transpose_and_quantise(n)
-
-        out_pool = ctx.enter_context(tc.tile_pool(name="out_pool", bufs=3))
+        out_pool = ctx.enter_context(tc.tile_pool(name="out_pool", bufs=4))
         side_pool = ctx.enter_context(tc.tile_pool(name="side_pool", bufs=3))
 
-        def times_table(out, bank, factor, table):
-            nc.vector.scalar_tensor_tensor(out=out, in0=bank, scalar=factor, in1=table, op0=MULT, op1=MULT)
+        def transpose_and_quantise(group):
+            x_words = x_tiles[group][:].bitcast(F32)
+            grouped = x_stage.tile([P, TILES, PASSES * P * PACK], BF16, align_bytes=64)
+            for i in range(TILES):
+                xt = psum_t.tile([P, PASSES * 2, P], F32)
+                for j in range(PASSES * 2):
+                    first = i * WORDS + j * P
+                    nc.tensor.transpose(out=xt[:, j, :], in_=x_words[:, first : first + P], identity=identity[:])
+                nc.scalar.copy(
+                    out=grouped[:, i, :].bitcast(F32).rearrange("p (g r u) -> p g r u", g=PASSES, u=2),
+                    in_=xt[:].rearrange("p (g u) r -> p g r u", u=2),
+                )
+            codes = x_stage.tile([P, TILES, PASSES, P], U32, align_bytes=64)
+            scales = x_stage.tile([P, TILES, PASSES, P], U8, align_bytes=64)
+            nc.vector.quantize_mx(
+                out=codes[:].rearrange("p i g r -> p (i g r)").bitcast(FP8X4),
+                scales=scales[:].rearrange("p i g r -> p (i g r)"),
+                in_=grouped[:].rearrange("p i c -> p (i c)"),
+            )
+            return codes, scales
 
-        def project(n, bank, col, width):
-            codes, scales = x_mx[n]
+        def project(x_mx, i, bank, col, width):
+            codes, scales = x_mx
             for g in range(PASSES):
-                tokens = slice(g * P, (g + 1) * P)
                 nc.tensor.matmul_mx(
                     out=bank,
-                    lhsT=codes[:, tokens].bitcast(FP8X4),
-                    lhsT_scale=scales[:, tokens],
+                    lhsT=codes[:, i, g, :].bitcast(FP8X4),
+                    lhsT_scale=scales[:, i, g, :],
                     rhs=w_codes[:, g, col : col + width].bitcast(FP8X4),
                     rhs_scale=w_scales[:, g, col : col + width],
                     start=(g == 0),
                     stop=(g == PASSES - 1),
                 )
 
+        def times_table(out, bank, factor, table):
+            nc.vector.scalar_tensor_tensor(out=out, in0=bank, scalar=factor, in1=table, op0=MULT, op1=MULT)
+
+        x_next = transpose_and_quantise(0)
         for group in range(N_GROUPS):
             b, s = divmod(group, GROUPS_PER_BATCH)
-            result = out_pool.tile([P, HEADS + 2, TILES, HEAD_DIM], F32)
+            x_now = x_next
+            if group + 1 < N_GROUPS:
+                x_next = transpose_and_quantise(group + 1)
+
+            banks_lower = []
+            banks_upper = []
+            for i in range(TILES):
+                bank_lower = psum_q.tile([P, HEADS, HALF], F32)
+                bank_upper = psum_q.tile([P, HEADS, HALF], F32)
+                project(x_now, i, bank_lower[:].rearrange("p h d -> p (h d)"), COL_LOWER, HEADS * HALF)
+                project(x_now, i, bank_upper[:].rearrange("p h d -> p (h d)"), COL_UPPER, HEADS * HALF)
+                banks_lower.append(bank_lower)
+                banks_upper.append(bank_upper)
             bank_k = psum_kv.tile([P, TILES, HEAD_DIM], F32)
             bank_v = psum_kv.tile([P, TILES, HEAD_DIM], F32)
-
             for i in range(TILES):
-                n = group * TILES + i
-                if n % AHEAD == 0:
-                    for later in range(n + AHEAD, min(n + 2 * AHEAD, N_TILES)):
-                        x_mx[later] = transpose_and_quantise(later)
+                project(x_now, i, bank_k[:, i, :], COL_K, HEAD_DIM)
+                project(x_now, i, bank_v[:, i, :], COL_V, HEAD_DIM)
 
-                bank_lower = psum_q.tile([P, HEADS * HALF], F32)
-                bank_upper = psum_q.tile([P, HEADS * HALF], F32)
-                project(n, bank_lower[:], COL_LOWER, HEADS * HALF)
-                project(n, bank_upper[:], COL_UPPER, HEADS * HALF)
-                project(n, bank_k[:, i, :], COL_K, HEAD_DIM)
-                project(n, bank_v[:, i, :], COL_V, HEAD_DIM)
-
-                lower = bank_lower[:].rearrange("p (h d) -> p h d", d=HALF)
-                upper = bank_upper[:].rearrange("p (h d) -> p h d", d=HALF)
-                side = side_pool.tile([P, HEADS, HEAD_DIM], F32)
+            result = out_pool.tile([P, HEADS + 2, TILES, HEAD_DIM], F32)
+            side = side_pool.tile([P, HEADS + 1, TILES, HEAD_DIM], F32)
+            for i in range(TILES):
+                lower = banks_lower[i][:]
+                upper = banks_upper[i][:]
                 times_table(result[:, 0:HEADS, i, LOWER], lower, Q_SCALE, over_heads(cos_sb[:, s, i, LOWER]))
-                times_table(side[:, :, UPPER], lower, Q_SCALE, over_heads(sin_sb[:, s, i, UPPER]))
+                times_table(side[:, 0:HEADS, i, UPPER], lower, Q_SCALE, over_heads(sin_sb[:, s, i, UPPER]))
                 times_table(result[:, 0:HEADS, i, UPPER], upper, Q_SCALE, over_heads(cos_sb[:, s, i, UPPER]))
-                times_table(side[:, :, LOWER], upper, -Q_SCALE, over_heads(sin_sb[:, s, i, LOWER]))
-                nc.gpsimd.tensor_tensor(
-                    out=result[:, 0:HEADS, i, :], in0=result[:, 0:HEADS, i, :], in1=side[:], op=ADD
-                )
-
-            side_k = side_pool.tile([P, TILES, HEAD_DIM], F32)
+                times_table(side[:, 0:HEADS, i, LOWER], upper, -Q_SCALE, over_heads(sin_sb[:, s, i, LOWER]))
             times_table(result[:, ROW_K, :, :], bank_k[:], 1.0, cos_sb[:, s, :, :])
-            times_table(side_k[:, :, LOWER], bank_k[:, :, UPPER], -1.0, sin_sb[:, s, :, LOWER])
-            times_table(side_k[:, :, UPPER], bank_k[:, :, LOWER], 1.0, sin_sb[:, s, :, UPPER])
-            nc.gpsimd.tensor_tensor(out=result[:, ROW_K, :, :], in0=result[:, ROW_K, :, :], in1=side_k[:], op=ADD)
+            times_table(side[:, ROW_K, :, LOWER], bank_k[:, :, UPPER], -1.0, sin_sb[:, s, :, LOWER])
+            times_table(side[:, ROW_K, :, UPPER], bank_k[:, :, LOWER], 1.0, sin_sb[:, s, :, UPPER])
             nc.scalar.copy(out=result[:, ROW_V, :, :], in_=bank_v[:])
+
+            adder = nc.vector if group % VECTOR_ADD_PERIOD == VECTOR_ADD_PERIOD - 1 else nc.gpsimd
+            rotated = result[:, 0 : HEADS + 1, :, :]
+            adder.tensor_tensor(out=rotated, in0=rotated, in1=side[:], op=ADD)
 
             positions = slice(s * GROUP, (s + 1) * GROUP)
             nc.sync.dma_start(

@@ -31,8 +31,6 @@ GROUP = TILES * P
 GROUPS_PER_BATCH = SEQ // GROUP
 N_GROUPS = BATCH * GROUPS_PER_BATCH
 
-VECTOR_ADD_PERIOD = 16
-
 COL_LOWER = 0
 COL_UPPER = HEADS * HALF
 COL_K = D_MODEL
@@ -63,8 +61,6 @@ def tile_multiqueryattention_pa_t_kernel(tc, x, sin, cos, w_qkv, q_rot, k_rot, v
 
         cos_sb = consts.tile([P, GROUPS_PER_BATCH, TILES, HEAD_DIM], BF16)
         sin_sb = consts.tile([P, GROUPS_PER_BATCH, TILES, HEAD_DIM], BF16)
-        nc.scalar.dma_start(out=cos_sb[:], in_=cos.rearrange("(s p i) d -> p s i d", p=P, i=TILES))
-        nc.scalar.dma_start(out=sin_sb[:], in_=sin.rearrange("(s p i) d -> p s i d", p=P, i=TILES))
 
         identity = consts.tile([P, P], F32)
         make_identity(nc, identity[:])
@@ -75,18 +71,27 @@ def tile_multiqueryattention_pa_t_kernel(tc, x, sin, cos, w_qkv, q_rot, k_rot, v
 
         with tc.tile_pool(name="w_stage", bufs=1) as w_stage:
             w_raw = w_stage.tile([P, PASSES, PACK, N_QKV], BF16)
-            for g in range(PASSES):
+            def load_w(g):
                 rows = w_qkv[g * K_PASS : (g + 1) * K_PASS, :]
                 nc.sync.dma_start(
                     out=w_raw[:, g, :, :].rearrange("p (u e) c -> p u e c", u=2),
                     in_=rows.rearrange("(u p e) c -> p u e c", u=2, e=2),
                 )
-            for group in range(N_GROUPS):
+
+            def load_x(group):
                 b, s = divmod(group, GROUPS_PER_BATCH)
                 x_sb = x_pool.tile([P, TILES * D_MODEL], BF16)
                 rows = x[b, s * GROUP : (s + 1) * GROUP, :]
                 nc.sync.dma_start(out=x_sb[:], in_=rows.rearrange("(p i) k -> p (i k)", i=TILES))
                 x_tiles.append(x_sb)
+
+            load_w(0)
+            load_w(1)
+            load_x(0)
+            for table_sb, table in ((cos_sb, cos), (sin_sb, sin)):
+                nc.sync.dma_start(out=table_sb[:], in_=table.rearrange("(s p i) d -> p s i d", p=P, i=TILES))
+            for group in range(1, N_GROUPS):
+                load_x(group)
 
             w_grouped = w_stage.tile([P, PASSES, N_QKV, PACK], BF16, align_bytes=64)
             for g in range(PASSES):
@@ -186,20 +191,27 @@ def tile_multiqueryattention_pa_t_kernel(tc, x, sin, cos, w_qkv, q_rot, k_rot, v
             times_table(side[:, ROW_K, :, UPPER], bank_k[:, :, LOWER], 1.0, sin_sb[:, s, :, UPPER])
             nc.scalar.copy(out=result[:, ROW_V, :, :], in_=bank_v[:])
 
-            adder = nc.vector if group % VECTOR_ADD_PERIOD == VECTOR_ADD_PERIOD - 1 else nc.gpsimd
-            rotated = result[:, 0 : HEADS + 1, :, :]
-            adder.tensor_tensor(out=rotated, in0=rotated, in1=side[:], op=ADD)
-
             positions = slice(s * GROUP, (s + 1) * GROUP)
-            nc.sync.dma_start(
-                out=q_rot[b, :, positions, :].rearrange("h (p i) d -> p h (i d)", i=TILES),
-                in_=result[:, 0:HEADS, :, :].rearrange("p h i d -> p h (i d)"),
-            )
-            nc.sync.dma_start(
-                out=k_rot[b, positions, :].rearrange("(p i) d -> p (i d)", i=TILES),
-                in_=result[:, ROW_K, :, :].rearrange("p i d -> p (i d)"),
-            )
-            nc.sync.dma_start(
-                out=v_out[b, positions, :].rearrange("(p i) d -> p (i d)", i=TILES),
-                in_=result[:, ROW_V, :, :].rearrange("p i d -> p (i d)"),
-            )
+
+            def store_row(row, out):
+                nc.sync.dma_start(
+                    out=out[b, positions, :].rearrange("(p i) d -> p (i d)", i=TILES),
+                    in_=result[:, row, :, :].rearrange("p i d -> p (i d)"),
+                )
+
+            if group + 1 < N_GROUPS:
+                pieces = [(nc.gpsimd, 0, HEADS + 1)]
+            else:
+                pieces = [(nc.vector, 0, HEADS // 2), (nc.vector, HEADS // 2, HEADS + 1)]
+                store_row(ROW_V, v_out)
+            for adder, first, last in pieces:
+                rotated = result[:, first:last, :, :]
+                adder.tensor_tensor(out=rotated, in0=rotated, in1=side[:, first:last, :, :], op=ADD)
+                heads = slice(first, min(last, HEADS))
+                nc.sync.dma_start(
+                    out=q_rot[b, heads, positions, :].rearrange("h (p i) d -> p h (i d)", i=TILES),
+                    in_=result[:, heads, :, :].rearrange("p h i d -> p h (i d)"),
+                )
+            store_row(ROW_K, k_rot)
+            if group + 1 < N_GROUPS:
+                store_row(ROW_V, v_out)

from contextlib import ExitStack

import concourse.mybir as mybir
from concourse.masks import make_identity

F32 = mybir.dt.float32
BF16 = mybir.dt.bfloat16
U32 = mybir.dt.uint32
U8 = mybir.dt.uint8
FP8X4 = mybir.dt.float8_e4m3fn_x4
MULT = mybir.AluOpType.mult
ADD = mybir.AluOpType.add

P = 128
BATCH = 4
SEQ = 1024
D_MODEL = 1024
HEADS = 8
HEAD_DIM = 128
HALF = HEAD_DIM // 2
Q_SCALE = HEAD_DIM**-0.5
N_QKV = D_MODEL + 2 * HEAD_DIM

PACK = 4
K_PASS = P * PACK
PASSES = D_MODEL // K_PASS
WORDS = D_MODEL // 2

TILES = 2
GROUP = TILES * P
GROUPS_PER_BATCH = SEQ // GROUP
N_GROUPS = BATCH * GROUPS_PER_BATCH

COL_LOWER = 0
COL_UPPER = HEADS * HALF
COL_K = D_MODEL
COL_V = D_MODEL + HEAD_DIM

ROW_K = HEADS
ROW_V = HEADS + 1

LOWER = slice(0, HALF)
UPPER = slice(HALF, HEAD_DIM)

FLOPS = 2 * BATCH * SEQ * D_MODEL * N_QKV


def over_heads(table_half):
    return table_half.unsqueeze(1).to_broadcast([P, HEADS, HALF])


def tile_multiqueryattention_pa_t_kernel(tc, x, sin, cos, w_qkv, q_rot, k_rot, v_out):
    nc = tc.nc
    with ExitStack() as ctx:
        consts = ctx.enter_context(tc.tile_pool(name="consts", bufs=1))
        x_pool = ctx.enter_context(tc.tile_pool(name="x_pool", bufs=N_GROUPS))
        x_stage = ctx.enter_context(tc.tile_pool(name="x_stage", bufs=3))
        psum_t = ctx.enter_context(tc.psum_pool(name="psum_t", bufs=TILES))
        psum_q = ctx.enter_context(tc.psum_pool(name="psum_q", bufs=2))
        psum_kv = ctx.enter_context(tc.psum_pool(name="psum_kv", bufs=1))

        cos_sb = consts.tile([P, GROUPS_PER_BATCH, TILES, HEAD_DIM], BF16)
        sin_sb = consts.tile([P, GROUPS_PER_BATCH, TILES, HEAD_DIM], BF16)

        identity = consts.tile([P, P], F32)
        make_identity(nc, identity[:])

        w_codes = consts.tile([P, PASSES, N_QKV], U32, align_bytes=64)
        w_scales = consts.tile([P, PASSES, N_QKV], U8, align_bytes=64)
        x_tiles = []

        with tc.tile_pool(name="w_stage", bufs=1) as w_stage:
            w_raw = w_stage.tile([P, PASSES, PACK, N_QKV], BF16)
            def load_w(g):
                rows = w_qkv[g * K_PASS : (g + 1) * K_PASS, :]
                nc.sync.dma_start(
                    out=w_raw[:, g, :, :].rearrange("p (u e) c -> p u e c", u=2),
                    in_=rows.rearrange("(u p e) c -> p u e c", u=2, e=2),
                )

            def load_x(group):
                b, s = divmod(group, GROUPS_PER_BATCH)
                x_sb = x_pool.tile([P, TILES * D_MODEL], BF16)
                rows = x[b, s * GROUP : (s + 1) * GROUP, :]
                nc.sync.dma_start(out=x_sb[:], in_=rows.rearrange("(p i) k -> p (i k)", i=TILES))
                x_tiles.append(x_sb)

            load_w(0)
            load_w(1)
            load_x(0)
            for table_sb, table in ((cos_sb, cos), (sin_sb, sin)):
                nc.sync.dma_start(out=table_sb[:], in_=table.rearrange("(s p i) d -> p s i d", p=P, i=TILES))
            for group in range(1, N_GROUPS):
                load_x(group)

            w_grouped = w_stage.tile([P, PASSES, N_QKV, PACK], BF16, align_bytes=64)
            for g in range(PASSES):
                q_halves = w_raw[:, g, :, 0:D_MODEL].rearrange("p t (h two d) -> p two h d t", two=2, d=HALF)
                nc.vector.tensor_copy(
                    out=w_grouped[:, g, COL_LOWER:COL_UPPER, :].rearrange("p (h d) t -> p h d t", d=HALF),
                    in_=q_halves[:, 0],
                )
                nc.scalar.copy(
                    out=w_grouped[:, g, COL_UPPER:COL_K, :].rearrange("p (h d) t -> p h d t", d=HALF),
                    in_=q_halves[:, 1],
                )
                nc.vector.tensor_copy(
                    out=w_grouped[:, g, COL_K:N_QKV, :],
                    in_=w_raw[:, g, :, COL_K:N_QKV].rearrange("p t c -> p c t"),
                )
                for cols in (slice(COL_LOWER, COL_UPPER), slice(COL_K, N_QKV), slice(COL_UPPER, COL_K)):
                    nc.vector.quantize_mx(
                        out=w_codes[:, g, cols].bitcast(FP8X4),
                        scales=w_scales[:, g, cols],
                        in_=w_grouped[:, g, cols, :].rearrange("p c t -> p (c t)"),
                    )

        out_pool = ctx.enter_context(tc.tile_pool(name="out_pool", bufs=4))
        side_pool = ctx.enter_context(tc.tile_pool(name="side_pool", bufs=3))

        def transpose_and_quantise(group):
            x_words = x_tiles[group][:].bitcast(F32)
            grouped = x_stage.tile([P, TILES, PASSES * P * PACK], BF16, align_bytes=64)
            for i in range(TILES):
                xt = psum_t.tile([P, PASSES * 2, P], F32)
                for j in range(PASSES * 2):
                    first = i * WORDS + j * P
                    nc.tensor.transpose(out=xt[:, j, :], in_=x_words[:, first : first + P], identity=identity[:])
                nc.scalar.copy(
                    out=grouped[:, i, :].bitcast(F32).rearrange("p (g r u) -> p g r u", g=PASSES, u=2),
                    in_=xt[:].rearrange("p (g u) r -> p g r u", u=2),
                )
            codes = x_stage.tile([P, TILES, PASSES, P], U32, align_bytes=64)
            scales = x_stage.tile([P, TILES, PASSES, P], U8, align_bytes=64)
            nc.vector.quantize_mx(
                out=codes[:].rearrange("p i g r -> p (i g r)").bitcast(FP8X4),
                scales=scales[:].rearrange("p i g r -> p (i g r)"),
                in_=grouped[:].rearrange("p i c -> p (i c)"),
            )
            return codes, scales

        def project(x_mx, i, bank, col, width):
            codes, scales = x_mx
            for g in range(PASSES):
                nc.tensor.matmul_mx(
                    out=bank,
                    lhsT=codes[:, i, g, :].bitcast(FP8X4),
                    lhsT_scale=scales[:, i, g, :],
                    rhs=w_codes[:, g, col : col + width].bitcast(FP8X4),
                    rhs_scale=w_scales[:, g, col : col + width],
                    start=(g == 0),
                    stop=(g == PASSES - 1),
                )

        def times_table(out, bank, factor, table):
            nc.vector.scalar_tensor_tensor(out=out, in0=bank, scalar=factor, in1=table, op0=MULT, op1=MULT)

        x_next = transpose_and_quantise(0)
        for group in range(N_GROUPS):
            b, s = divmod(group, GROUPS_PER_BATCH)
            x_now = x_next
            if group + 1 < N_GROUPS:
                x_next = transpose_and_quantise(group + 1)

            banks_lower = []
            banks_upper = []
            for i in range(TILES):
                bank_lower = psum_q.tile([P, HEADS, HALF], F32)
                bank_upper = psum_q.tile([P, HEADS, HALF], F32)
                project(x_now, i, bank_lower[:].rearrange("p h d -> p (h d)"), COL_LOWER, HEADS * HALF)
                project(x_now, i, bank_upper[:].rearrange("p h d -> p (h d)"), COL_UPPER, HEADS * HALF)
                banks_lower.append(bank_lower)
                banks_upper.append(bank_upper)
            bank_k = psum_kv.tile([P, TILES, HEAD_DIM], F32)
            bank_v = psum_kv.tile([P, TILES, HEAD_DIM], F32)
            for i in range(TILES):
                project(x_now, i, bank_k[:, i, :], COL_K, HEAD_DIM)
                project(x_now, i, bank_v[:, i, :], COL_V, HEAD_DIM)

            result = out_pool.tile([P, HEADS + 2, TILES, HEAD_DIM], F32)
            side = side_pool.tile([P, HEADS + 1, TILES, HEAD_DIM], F32)
            for i in range(TILES):
                lower = banks_lower[i][:]
                upper = banks_upper[i][:]
                times_table(result[:, 0:HEADS, i, LOWER], lower, Q_SCALE, over_heads(cos_sb[:, s, i, LOWER]))
                times_table(side[:, 0:HEADS, i, UPPER], lower, Q_SCALE, over_heads(sin_sb[:, s, i, UPPER]))
                times_table(result[:, 0:HEADS, i, UPPER], upper, Q_SCALE, over_heads(cos_sb[:, s, i, UPPER]))
                times_table(side[:, 0:HEADS, i, LOWER], upper, -Q_SCALE, over_heads(sin_sb[:, s, i, LOWER]))
            times_table(result[:, ROW_K, :, :], bank_k[:], 1.0, cos_sb[:, s, :, :])
            times_table(side[:, ROW_K, :, LOWER], bank_k[:, :, UPPER], -1.0, sin_sb[:, s, :, LOWER])
            times_table(side[:, ROW_K, :, UPPER], bank_k[:, :, LOWER], 1.0, sin_sb[:, s, :, UPPER])
            nc.scalar.copy(out=result[:, ROW_V, :, :], in_=bank_v[:])

            positions = slice(s * GROUP, (s + 1) * GROUP)

            def store_row(row, out):
                nc.sync.dma_start(
                    out=out[b, positions, :].rearrange("(p i) d -> p (i d)", i=TILES),
                    in_=result[:, row, :, :].rearrange("p i d -> p (i d)"),
                )

            if group + 1 < N_GROUPS:
                pieces = [(nc.gpsimd, 0, HEADS + 1)]
            else:
                pieces = [(nc.vector, 0, HEADS // 2), (nc.vector, HEADS // 2, HEADS + 1)]
                store_row(ROW_V, v_out)
            for adder, first, last in pieces:
                rotated = result[:, first:last, :, :]
                adder.tensor_tensor(out=rotated, in0=rotated, in1=side[:, first:last, :, :], op=ADD)
                heads = slice(first, min(last, HEADS))
                nc.sync.dma_start(
                    out=q_rot[b, heads, positions, :].rearrange("h (p i) d -> p h (i d)", i=TILES),
                    in_=result[:, heads, :, :].rearrange("p h i d -> p h (i d)"),
                )
            store_row(ROW_K, k_rot)
            if group + 1 < N_GROUPS:
                store_row(ROW_V, v_out)
